import numpy as np
import ml_dtypes

BF16 = ml_dtypes.bfloat16


def bf(x):
    return np.asarray(x, np.float32).astype(BF16)


def f32(x):
    return np.asarray(x, np.float32)


def f64(x):
    return np.asarray(x).astype(np.float64)


def striped(idx):
    return np.tile(idx.reshape(-1, 16).T, (8, 1))


NB, INC, OUTC, S, OUTN, MAXD, C, N = 8, 128, 128, 256, 256, 4, 1024, 1024


def setup_inputs():
    return {"x": f32(np.random.standard_normal((C, S))), "weight": f32(np.random.standard_normal((INC, S))), "mask_weight": f32(np.random.standard_normal((1, N))), "ct_weight": bf(np.random.standard_normal((INC, OUTC)) / np.sqrt(INC)), "ct_bias": f32(0.1 * np.random.standard_normal((OUTC, 1))), "bias": f32(0.2 * np.random.standard_normal((OUTC, OUTN))), "offs": striped(np.concatenate([np.random.permutation(S) for _ in range(MAXD)]))}


def reference(x, weight, mask_weight, ct_weight, ct_bias, bias, offs):
    idx = offs[:16].T.reshape(-1)
    feat = f64(x) * np.tile(f64(weight), (NB, 1))
    msg = feat[:, idx] * (f64(mask_weight) / MAXD)
    pooled = msg.reshape(C, MAXD, OUTN).sum(axis=1)
    y = np.einsum('im,bio->bmo', f64(ct_weight), pooled.reshape(NB, INC, OUTN))
    y = y + f64(ct_bias)[None, :, :] + f64(bias)[None, :, :]
    return y.reshape(NB * OUTC, OUTN)

@@ -1,0 +1,72 @@
+import concourse.mybir as mybir
+
+F32 = mybir.dt.float32
+BF16 = mybir.dt.bfloat16
+U16 = mybir.dt.uint16
+MULT = mybir.AluOpType.mult
+ADD = mybir.AluOpType.add
+COPY = mybir.ActivationFunctionType.Copy
+IDENTITY = mybir.ActivationFunctionType.Identity
+
+P = 128
+SAMPLES = 8
+NODES_IN = 256
+NODES_OUT = 256
+NEIGHBOURS = 4
+EDGES = NEIGHBOURS * NODES_OUT
+PIECE_COLS = NODES_OUT // 16
+
+FLOPS = 2 * SAMPLES * P * P * NODES_OUT
+
+
+def tile_fgl_kernel(tc, x, weight, mask_weight, ct_weight, ct_bias, bias, offs, out):
+    nc = tc.nc
+    with (
+        tc.tile_pool(name="held", bufs=1) as held,
+        tc.tile_pool(name="work", bufs=2) as work,
+        tc.psum_pool(name="psum", bufs=2) as psum,
+    ):
+        offsets = held.tile([P, EDGES // 16], U16, name="offsets")
+        nc.sync.dma_start(offsets[:], offs)
+        node_weight = held.tile([P, NODES_IN], F32, name="node_weight")
+        nc.scalar.dma_start(node_weight[:], weight)
+        x_all = held.tile([P, SAMPLES, NODES_IN], F32, name="x_all")
+        nc.sync.dma_start(x_all[:, 0, :], x[0:P, :])
+        edge_weight = held.tile([P, EDGES], F32, name="edge_weight")
+        nc.scalar.dma_start(edge_weight[:], mask_weight.broadcast_to([P, EDGES]))
+        for b in range(1, SAMPLES):
+            nc.sync.dma_start(x_all[:, b, :], x[b * P : (b + 1) * P, :])
+        mix_weight = held.tile([P, P], BF16, name="mix_weight")
+        nc.scalar.dma_start(mix_weight[:], ct_weight)
+        node_bias = held.tile([P, NODES_OUT], F32, name="node_bias")
+        nc.scalar.dma_start(node_bias[:], bias)
+        channel_bias = held.tile([P, 1], F32, name="channel_bias")
+        nc.scalar.dma_start(channel_bias[:], ct_bias)
+
+        bias_sum = held.tile([P, NODES_OUT], F32, name="bias_sum")
+        nc.scalar.activation(bias_sum[:], node_bias[:], IDENTITY, bias=channel_bias[:, 0:1])
+
+        for b in range(SAMPLES):
+            feat = work.tile([P, NODES_IN], F32, name="feat")
+            nc.vector.tensor_tensor(feat[:], x_all[:, b, :], node_weight[:], MULT)
+
+            msg = work.tile([P, EDGES], F32, name="msg")
+            for d in range(NEIGHBOURS):
+                piece = slice(d * NODES_OUT, (d + 1) * NODES_OUT)
+                looked_up = feat[:].indirect(offsets[:, d * PIECE_COLS : (d + 1) * PIECE_COLS])
+                nc.vector.tensor_tensor(msg[:, piece], looked_up, edge_weight[:, piece], MULT)
+
+            pairs = work.tile([P, 2 * NODES_OUT], F32, name="pairs")
+            nc.vector.tensor_tensor(pairs[:], msg[:, : 2 * NODES_OUT], msg[:, 2 * NODES_OUT :], ADD)
+            total = work.tile([P, NODES_OUT], F32, name="total")
+            nc.vector.tensor_tensor(total[:], pairs[:, :NODES_OUT], pairs[:, NODES_OUT:], ADD)
+
+            pooled = work.tile([P, NODES_OUT], BF16, name="pooled")
+            nc.scalar.activation(pooled[:], total[:], COPY, scale=1.0 / NEIGHBOURS)
+
+            mixed = psum.tile([P, NODES_OUT], F32, name="mixed")
+            nc.tensor.matmul(mixed[:], mix_weight[:], pooled[:], start=True, stop=True)
+
+            result = work.tile([P, NODES_OUT], F32, name="result")
+            nc.vector.tensor_tensor(result[:], mixed[:], bias_sum[:], ADD)
+            nc.sync.dma_start(out[b * P : (b + 1) * P, :], result[:])

@@ -1,4 +1,5 @@
 import concourse.mybir as mybir
+from concourse.masks import make_identity
 
 F32 = mybir.dt.float32
 BF16 = mybir.dt.bfloat16
@@ -24,6 +25,7 @@ def tile_fgl_kernel(tc, x, weight, mask_weight, ct_weight, ct_bias, bias, offs, 
     with (
         tc.tile_pool(name="held", bufs=1) as held,
         tc.tile_pool(name="work", bufs=2) as work,
+        tc.tile_pool(name="msgs", bufs=2 * NEIGHBOURS) as msgs,
         tc.psum_pool(name="psum", bufs=2) as psum,
     ):
         offsets = held.tile([P, EDGES // 16], U16, name="offsets")
@@ -46,20 +48,21 @@ def tile_fgl_kernel(tc, x, weight, mask_weight, ct_weight, ct_bias, bias, offs, 
         bias_sum = held.tile([P, NODES_OUT], F32, name="bias_sum")
         nc.scalar.activation(bias_sum[:], node_bias[:], IDENTITY, bias=channel_bias[:, 0:1])
 
+        identity = held.tile([P, P], F32, name="identity")
+        make_identity(nc, identity[:])
+
         for b in range(SAMPLES):
             feat = work.tile([P, NODES_IN], F32, name="feat")
             nc.vector.tensor_tensor(feat[:], x_all[:, b, :], node_weight[:], MULT)
 
-            msg = work.tile([P, EDGES], F32, name="msg")
+            total = psum.tile([P, NODES_OUT], F32, name="total")
             for d in range(NEIGHBOURS):
-                piece = slice(d * NODES_OUT, (d + 1) * NODES_OUT)
+                msg = msgs.tile([P, NODES_OUT], F32, name="msg")
                 looked_up = feat[:].indirect(offsets[:, d * PIECE_COLS : (d + 1) * PIECE_COLS])
-                nc.vector.tensor_tensor(msg[:, piece], looked_up, edge_weight[:, piece], MULT)
-
-            pairs = work.tile([P, 2 * NODES_OUT], F32, name="pairs")
-            nc.vector.tensor_tensor(pairs[:], msg[:, : 2 * NODES_OUT], msg[:, 2 * NODES_OUT :], ADD)
-            total = work.tile([P, NODES_OUT], F32, name="total")
-            nc.vector.tensor_tensor(total[:], pairs[:, :NODES_OUT], pairs[:, NODES_OUT:], ADD)
+                nc.vector.tensor_tensor(
+                    msg[:], looked_up, edge_weight[:, d * NODES_OUT : (d + 1) * NODES_OUT], MULT
+                )
+                nc.tensor.matmul(total[:], identity[:], msg[:], start=(d == 0), stop=(d == NEIGHBOURS - 1))
 
             pooled = work.tile([P, NODES_OUT], BF16, name="pooled")
             nc.scalar.activation(pooled[:], total[:], COPY, scale=1.0 / NEIGHBOURS)

@@ -24,9 +24,9 @@ def tile_fgl_kernel(tc, x, weight, mask_weight, ct_weight, ct_bias, bias, offs, 
     nc = tc.nc
     with (
         tc.tile_pool(name="held", bufs=1) as held,
-        tc.tile_pool(name="work", bufs=2) as work,
-        tc.tile_pool(name="msgs", bufs=2 * NEIGHBOURS) as msgs,
-        tc.psum_pool(name="psum", bufs=2) as psum,
+        tc.tile_pool(name="work", bufs=4) as work,
+        tc.tile_pool(name="msgs", bufs=4 * NEIGHBOURS) as msgs,
+        tc.psum_pool(name="psum", bufs=4) as psum,
     ):
         offsets = held.tile([P, EDGES // 16], U16, name="offsets")
         nc.sync.dma_start(offsets[:], offs)
@@ -35,15 +35,18 @@ def tile_fgl_kernel(tc, x, weight, mask_weight, ct_weight, ct_bias, bias, offs, 
         x_all = held.tile([P, SAMPLES, NODES_IN], F32, name="x_all")
         nc.sync.dma_start(x_all[:, 0, :], x[0:P, :])
         edge_weight = held.tile([P, EDGES], F32, name="edge_weight")
-        nc.scalar.dma_start(edge_weight[:], mask_weight.broadcast_to([P, EDGES]))
-        for b in range(1, SAMPLES):
-            nc.sync.dma_start(x_all[:, b, :], x[b * P : (b + 1) * P, :])
+        for d in range(NEIGHBOURS):
+            piece = slice(d * NODES_OUT, (d + 1) * NODES_OUT)
+            queue = nc.scalar if d % 2 == 0 else nc.sync
+            queue.dma_start(edge_weight[:, piece], mask_weight[:, piece].broadcast_to([P, NODES_OUT]))
         mix_weight = held.tile([P, P], BF16, name="mix_weight")
         nc.scalar.dma_start(mix_weight[:], ct_weight)
         node_bias = held.tile([P, NODES_OUT], F32, name="node_bias")
         nc.scalar.dma_start(node_bias[:], bias)
         channel_bias = held.tile([P, 1], F32, name="channel_bias")
         nc.scalar.dma_start(channel_bias[:], ct_bias)
+        for b in range(1, SAMPLES):
+            nc.sync.dma_start(x_all[:, b, :], x[b * P : (b + 1) * P, :])
 
         bias_sum = held.tile([P, NODES_OUT], F32, name="bias_sum")
         nc.scalar.activation(bias_sum[:], node_bias[:], IDENTITY, bias=channel_bias[:, 0:1])
@@ -53,7 +56,7 @@ def tile_fgl_kernel(tc, x, weight, mask_weight, ct_weight, ct_bias, bias, offs, 
 
         for b in range(SAMPLES):
             feat = work.tile([P, NODES_IN], F32, name="feat")
-            nc.vector.tensor_tensor(feat[:], x_all[:, b, :], node_weight[:], MULT)
+            nc.gpsimd.tensor_tensor(feat[:], x_all[:, b, :], node_weight[:], MULT)
 
             total = psum.tile([P, NODES_OUT], F32, name="total")
             for d in range(NEIGHBOURS):

@@ -15,7 +15,10 @@ NODES_IN = 256
 NODES_OUT = 256
 NEIGHBOURS = 4
 EDGES = NEIGHBOURS * NODES_OUT
-PIECE_COLS = NODES_OUT // 16
+OFFSETS_PER_COLUMN = 16
+PIECE_COLUMNS = NODES_OUT // OFFSETS_PER_COLUMN
+
+SAMPLES_IN_FLIGHT = 4
 
 FLOPS = 2 * SAMPLES * P * P * NODES_OUT
 
@@ -24,11 +27,11 @@ def tile_fgl_kernel(tc, x, weight, mask_weight, ct_weight, ct_bias, bias, offs, 
     nc = tc.nc
     with (
         tc.tile_pool(name="held", bufs=1) as held,
-        tc.tile_pool(name="work", bufs=4) as work,
-        tc.tile_pool(name="msgs", bufs=4 * NEIGHBOURS) as msgs,
-        tc.psum_pool(name="psum", bufs=4) as psum,
+        tc.tile_pool(name="work", bufs=SAMPLES_IN_FLIGHT) as work,
+        tc.tile_pool(name="msgs", bufs=SAMPLES_IN_FLIGHT * NEIGHBOURS) as msgs,
+        tc.psum_pool(name="psum", bufs=SAMPLES_IN_FLIGHT) as psum,
     ):
-        offsets = held.tile([P, EDGES // 16], U16, name="offsets")
+        offsets = held.tile([P, EDGES // OFFSETS_PER_COLUMN], U16, name="offsets")
         nc.sync.dma_start(offsets[:], offs)
         node_weight = held.tile([P, NODES_IN], F32, name="node_weight")
         nc.scalar.dma_start(node_weight[:], weight)
@@ -56,12 +59,12 @@ def tile_fgl_kernel(tc, x, weight, mask_weight, ct_weight, ct_bias, bias, offs, 
 
         for b in range(SAMPLES):
             feat = work.tile([P, NODES_IN], F32, name="feat")
-            nc.gpsimd.tensor_tensor(feat[:], x_all[:, b, :], node_weight[:], MULT)
+            nc.vector.tensor_tensor(feat[:], x_all[:, b, :], node_weight[:], MULT)
 
             total = psum.tile([P, NODES_OUT], F32, name="total")
             for d in range(NEIGHBOURS):
                 msg = msgs.tile([P, NODES_OUT], F32, name="msg")
-                looked_up = feat[:].indirect(offsets[:, d * PIECE_COLS : (d + 1) * PIECE_COLS])
+                looked_up = feat[:].indirect(offsets[:, d * PIECE_COLUMNS : (d + 1) * PIECE_COLUMNS])
                 nc.vector.tensor_tensor(
                     msg[:], looked_up, edge_weight[:, d * NODES_OUT : (d + 1) * NODES_OUT], MULT
                 )
@@ -72,7 +75,6 @@ def tile_fgl_kernel(tc, x, weight, mask_weight, ct_weight, ct_bias, bias, offs, 
 
             mixed = psum.tile([P, NODES_OUT], F32, name="mixed")
             nc.tensor.matmul(mixed[:], mix_weight[:], pooled[:], start=True, stop=True)
-
             result = work.tile([P, NODES_OUT], F32, name="result")
             nc.vector.tensor_tensor(result[:], mixed[:], bias_sum[:], ADD)
             nc.sync.dma_start(out[b * P : (b + 1) * P, :], result[:])

@@ -16,7 +16,6 @@ NODES_OUT = 256
 NEIGHBOURS = 4
 EDGES = NEIGHBOURS * NODES_OUT
 OFFSETS_PER_COLUMN = 16
-PIECE_COLUMNS = NODES_OUT // OFFSETS_PER_COLUMN
 
 SAMPLES_IN_FLIGHT = 4
 
@@ -28,6 +27,7 @@ def tile_fgl_kernel(tc, x, weight, mask_weight, ct_weight, ct_bias, bias, offs, 
     with (
         tc.tile_pool(name="held", bufs=1) as held,
         tc.tile_pool(name="work", bufs=SAMPLES_IN_FLIGHT) as work,
+        tc.tile_pool(name="results", bufs=SAMPLES + 1) as results,
         tc.tile_pool(name="msgs", bufs=SAMPLES_IN_FLIGHT * NEIGHBOURS) as msgs,
         tc.psum_pool(name="psum", bufs=SAMPLES_IN_FLIGHT) as psum,
     ):
@@ -61,20 +61,26 @@ def tile_fgl_kernel(tc, x, weight, mask_weight, ct_weight, ct_bias, bias, offs, 
             feat = work.tile([P, NODES_IN], F32, name="feat")
             nc.vector.tensor_tensor(feat[:], x_all[:, b, :], node_weight[:], MULT)
 
-            total = psum.tile([P, NODES_OUT], F32, name="total")
-            for d in range(NEIGHBOURS):
-                msg = msgs.tile([P, NODES_OUT], F32, name="msg")
-                looked_up = feat[:].indirect(offsets[:, d * PIECE_COLUMNS : (d + 1) * PIECE_COLUMNS])
-                nc.vector.tensor_tensor(
-                    msg[:], looked_up, edge_weight[:, d * NODES_OUT : (d + 1) * NODES_OUT], MULT
-                )
-                nc.tensor.matmul(total[:], identity[:], msg[:], start=(d == 0), stop=(d == NEIGHBOURS - 1))
+            halves = 2 if b == SAMPLES - 1 else 1
+            width = NODES_OUT // halves
+            for first in range(0, NODES_OUT, width):
+                total = psum.tile([P, NODES_OUT], F32, name="total")
+                for d in range(NEIGHBOURS):
+                    entry = d * NODES_OUT + first
+                    msg = msgs.tile([P, NODES_OUT], F32, name="msg")
+                    looked_up = feat[:].indirect(
+                        offsets[:, entry // OFFSETS_PER_COLUMN : (entry + width) // OFFSETS_PER_COLUMN]
+                    )
+                    nc.vector.tensor_tensor(msg[:, 0:width], looked_up, edge_weight[:, entry : entry + width], MULT)
+                    nc.tensor.matmul(
+                        total[:, 0:width], identity[:], msg[:, 0:width], start=(d == 0), stop=(d == NEIGHBOURS - 1)
+                    )
 
-            pooled = work.tile([P, NODES_OUT], BF16, name="pooled")
-            nc.scalar.activation(pooled[:], total[:], COPY, scale=1.0 / NEIGHBOURS)
+                pooled = work.tile([P, NODES_OUT], BF16, name="pooled")
+                nc.scalar.activation(pooled[:, 0:width], total[:, 0:width], COPY, scale=1.0 / NEIGHBOURS)
 
-            mixed = psum.tile([P, NODES_OUT], F32, name="mixed")
-            nc.tensor.matmul(mixed[:], mix_weight[:], pooled[:], start=True, stop=True)
-            result = work.tile([P, NODES_OUT], F32, name="result")
-            nc.vector.tensor_tensor(result[:], mixed[:], bias_sum[:], ADD)
-            nc.sync.dma_start(out[b * P : (b + 1) * P, :], result[:])
+                mixed = psum.tile([P, NODES_OUT], F32, name="mixed")
+                nc.tensor.matmul(mixed[:, 0:width], mix_weight[:], pooled[:, 0:width], start=True, stop=True)
+                result = results.tile([P, NODES_OUT], F32, name="result")
+                nc.vector.tensor_tensor(result[:, 0:width], mixed[:, 0:width], bias_sum[:, first : first + width], ADD)
+                nc.sync.dma_start(out[b * P : (b + 1) * P, first : first + width], result[:, 0:width])

@@ -38,10 +38,11 @@ def tile_fgl_kernel(tc, x, weight, mask_weight, ct_weight, ct_bias, bias, offs, 
         x_all = held.tile([P, SAMPLES, NODES_IN], F32, name="x_all")
         nc.sync.dma_start(x_all[:, 0, :], x[0:P, :])
         edge_weight = held.tile([P, EDGES], F32, name="edge_weight")
+        half = NODES_OUT // 2
         for d in range(NEIGHBOURS):
-            piece = slice(d * NODES_OUT, (d + 1) * NODES_OUT)
-            queue = nc.scalar if d % 2 == 0 else nc.sync
-            queue.dma_start(edge_weight[:, piece], mask_weight[:, piece].broadcast_to([P, NODES_OUT]))
+            for k, queue in enumerate((nc.scalar, nc.sync)):
+                piece = slice(d * NODES_OUT + k * half, d * NODES_OUT + (k + 1) * half)
+                queue.dma_start(edge_weight[:, piece], mask_weight[:, piece].broadcast_to([P, half]))
         mix_weight = held.tile([P, P], BF16, name="mix_weight")
         nc.scalar.dma_start(mix_weight[:], ct_weight)
         node_bias = held.tile([P, NODES_OUT], F32, name="node_bias")

@@ -17,6 +17,9 @@ NEIGHBOURS = 4
 EDGES = NEIGHBOURS * NODES_OUT
 OFFSETS_PER_COLUMN = 16
 
+VECTOR_BIASES = 4
+OUTPUT_BANKS = VECTOR_BIASES + 1
+PSUM_BANKS = 8
 SAMPLES_IN_FLIGHT = 4
 
 FLOPS = 2 * SAMPLES * P * P * NODES_OUT
@@ -26,10 +29,12 @@ def tile_fgl_kernel(tc, x, weight, mask_weight, ct_weight, ct_bias, bias, offs, 
     nc = tc.nc
     with (
         tc.tile_pool(name="held", bufs=1) as held,
+        tc.tile_pool(name="windows", bufs=2) as windows,
         tc.tile_pool(name="work", bufs=SAMPLES_IN_FLIGHT) as work,
         tc.tile_pool(name="results", bufs=SAMPLES + 1) as results,
-        tc.tile_pool(name="msgs", bufs=SAMPLES_IN_FLIGHT * NEIGHBOURS) as msgs,
-        tc.psum_pool(name="psum", bufs=SAMPLES_IN_FLIGHT) as psum,
+        tc.tile_pool(name="msgs", bufs=(SAMPLES + 1) * NEIGHBOURS) as msgs,
+        tc.psum_pool(name="sums", bufs=PSUM_BANKS - OUTPUT_BANKS) as sums,
+        tc.psum_pool(name="outputs", bufs=OUTPUT_BANKS) as outputs,
     ):
         offsets = held.tile([P, EDGES // OFFSETS_PER_COLUMN], U16, name="offsets")
         nc.sync.dma_start(offsets[:], offs)
@@ -59,13 +64,13 @@ def tile_fgl_kernel(tc, x, weight, mask_weight, ct_weight, ct_bias, bias, offs, 
         make_identity(nc, identity[:])
 
         for b in range(SAMPLES):
-            feat = work.tile([P, NODES_IN], F32, name="feat")
+            feat = windows.tile([P, NODES_IN], F32, name="feat")
             nc.vector.tensor_tensor(feat[:], x_all[:, b, :], node_weight[:], MULT)
 
             halves = 2 if b == SAMPLES - 1 else 1
             width = NODES_OUT // halves
             for first in range(0, NODES_OUT, width):
-                total = psum.tile([P, NODES_OUT], F32, name="total")
+                total = sums.tile([P, NODES_OUT], F32, name="total")
                 for d in range(NEIGHBOURS):
                     entry = d * NODES_OUT + first
                     msg = msgs.tile([P, NODES_OUT], F32, name="msg")
@@ -80,8 +85,14 @@ def tile_fgl_kernel(tc, x, weight, mask_weight, ct_weight, ct_bias, bias, offs, 
                 pooled = work.tile([P, NODES_OUT], BF16, name="pooled")
                 nc.scalar.activation(pooled[:, 0:width], total[:, 0:width], COPY, scale=1.0 / NEIGHBOURS)
 
-                mixed = psum.tile([P, NODES_OUT], F32, name="mixed")
-                nc.tensor.matmul(mixed[:, 0:width], mix_weight[:], pooled[:, 0:width], start=True, stop=True)
+                mixed = outputs.tile([P, NODES_OUT], F32, name="mixed")
                 result = results.tile([P, NODES_OUT], F32, name="result")
-                nc.vector.tensor_tensor(result[:, 0:width], mixed[:, 0:width], bias_sum[:, first : first + width], ADD)
+                nodes = slice(first, first + width)
+                if b < SAMPLES - VECTOR_BIASES:
+                    nc.tensor.matmul(mixed[:, 0:width], mix_weight[:], pooled[:, 0:width], start=True, stop=False)
+                    nc.tensor.matmul(mixed[:, 0:width], identity[:], bias_sum[:, nodes], start=False, stop=True)
+                    nc.scalar.activation(result[:, 0:width], mixed[:, 0:width], COPY)
+                else:
+                    nc.tensor.matmul(mixed[:, 0:width], mix_weight[:], pooled[:, 0:width], start=True, stop=True)
+                    nc.vector.tensor_tensor(result[:, 0:width], mixed[:, 0:width], bias_sum[:, nodes], ADD)
                 nc.sync.dma_start(out[b * P : (b + 1) * P, first : first + width], result[:, 0:width])

@@ -17,7 +17,7 @@ NEIGHBOURS = 4
 EDGES = NEIGHBOURS * NODES_OUT
 OFFSETS_PER_COLUMN = 16
 
-VECTOR_BIASES = 4
+VECTOR_BIASES = 5
 OUTPUT_BANKS = VECTOR_BIASES + 1
 PSUM_BANKS = 8
 SAMPLES_IN_FLIGHT = 4
@@ -57,9 +57,6 @@ def tile_fgl_kernel(tc, x, weight, mask_weight, ct_weight, ct_bias, bias, offs, 
         for b in range(1, SAMPLES):
             nc.sync.dma_start(x_all[:, b, :], x[b * P : (b + 1) * P, :])
 
-        bias_sum = held.tile([P, NODES_OUT], F32, name="bias_sum")
-        nc.scalar.activation(bias_sum[:], node_bias[:], IDENTITY, bias=channel_bias[:, 0:1])
-
         identity = held.tile([P, P], F32, name="identity")
         make_identity(nc, identity[:])
 
@@ -90,9 +87,11 @@ def tile_fgl_kernel(tc, x, weight, mask_weight, ct_weight, ct_bias, bias, offs, 
                 nodes = slice(first, first + width)
                 if b < SAMPLES - VECTOR_BIASES:
                     nc.tensor.matmul(mixed[:, 0:width], mix_weight[:], pooled[:, 0:width], start=True, stop=False)
-                    nc.tensor.matmul(mixed[:, 0:width], identity[:], bias_sum[:, nodes], start=False, stop=True)
-                    nc.scalar.activation(result[:, 0:width], mixed[:, 0:width], COPY)
+                    nc.tensor.matmul(mixed[:, 0:width], identity[:], node_bias[:, nodes], start=False, stop=True)
+                    nc.scalar.activation(result[:, 0:width], mixed[:, 0:width], IDENTITY, bias=channel_bias[:, 0:1])
                 else:
                     nc.tensor.matmul(mixed[:, 0:width], mix_weight[:], pooled[:, 0:width], start=True, stop=True)
-                    nc.vector.tensor_tensor(result[:, 0:width], mixed[:, 0:width], bias_sum[:, nodes], ADD)
+                    nc.vector.scalar_tensor_tensor(
+                        result[:, 0:width], mixed[:, 0:width], channel_bias[:, 0:1], node_bias[:, nodes], ADD, ADD
+                    )
                 nc.sync.dma_start(out[b * P : (b + 1) * P, first : first + width], result[:, 0:width])

@@ -43,19 +43,19 @@ def tile_fgl_kernel(tc, x, weight, mask_weight, ct_weight, ct_bias, bias, offs, 
         x_all = held.tile([P, SAMPLES, NODES_IN], F32, name="x_all")
         nc.sync.dma_start(x_all[:, 0, :], x[0:P, :])
         edge_weight = held.tile([P, EDGES], F32, name="edge_weight")
-        half = NODES_OUT // 2
         for d in range(NEIGHBOURS):
-            for k, queue in enumerate((nc.scalar, nc.sync)):
-                piece = slice(d * NODES_OUT + k * half, d * NODES_OUT + (k + 1) * half)
-                queue.dma_start(edge_weight[:, piece], mask_weight[:, piece].broadcast_to([P, half]))
+            queue = nc.scalar if d % 2 == 0 else nc.sync
+            piece = slice(d * NODES_OUT, (d + 1) * NODES_OUT)
+            queue.dma_start(edge_weight[:, piece], mask_weight[:, piece].broadcast_to([P, NODES_OUT]))
         mix_weight = held.tile([P, P], BF16, name="mix_weight")
         nc.scalar.dma_start(mix_weight[:], ct_weight)
         node_bias = held.tile([P, NODES_OUT], F32, name="node_bias")
         nc.scalar.dma_start(node_bias[:], bias)
         channel_bias = held.tile([P, 1], F32, name="channel_bias")
         nc.scalar.dma_start(channel_bias[:], ct_bias)
-        for b in range(1, SAMPLES):
-            nc.sync.dma_start(x_all[:, b, :], x[b * P : (b + 1) * P, :])
+        for first, last in ((1, 2), (2, 4), (4, SAMPLES)):
+            rows = x[first * P : last * P, :].rearrange("(b p) s -> p b s", p=P)
+            nc.sync.dma_start(x_all[:, first:last, :], rows)
 
         identity = held.tile([P, P], F32, name="identity")
         make_identity(nc, identity[:])

@@ -36,12 +36,12 @@ def tile_fgl_kernel(tc, x, weight, mask_weight, ct_weight, ct_bias, bias, offs, 
         tc.psum_pool(name="sums", bufs=PSUM_BANKS - OUTPUT_BANKS) as sums,
         tc.psum_pool(name="outputs", bufs=OUTPUT_BANKS) as outputs,
     ):
-        offsets = held.tile([P, EDGES // OFFSETS_PER_COLUMN], U16, name="offsets")
-        nc.sync.dma_start(offsets[:], offs)
         node_weight = held.tile([P, NODES_IN], F32, name="node_weight")
         nc.scalar.dma_start(node_weight[:], weight)
         x_all = held.tile([P, SAMPLES, NODES_IN], F32, name="x_all")
         nc.sync.dma_start(x_all[:, 0, :], x[0:P, :])
+        offsets = held.tile([P, EDGES // OFFSETS_PER_COLUMN], U16, name="offsets")
+        nc.sync.dma_start(offsets[:], offs)
         edge_weight = held.tile([P, EDGES], F32, name="edge_weight")
         for d in range(NEIGHBOURS):
             queue = nc.scalar if d % 2 == 0 else nc.sync

import concourse.mybir as mybir
from concourse.masks import make_identity

F32 = mybir.dt.float32
BF16 = mybir.dt.bfloat16
U16 = mybir.dt.uint16
MULT = mybir.AluOpType.mult
ADD = mybir.AluOpType.add
COPY = mybir.ActivationFunctionType.Copy
IDENTITY = mybir.ActivationFunctionType.Identity

P = 128
SAMPLES = 8
NODES_IN = 256
NODES_OUT = 256
NEIGHBOURS = 4
EDGES = NEIGHBOURS * NODES_OUT
OFFSETS_PER_COLUMN = 16

VECTOR_BIASES = 5
OUTPUT_BANKS = VECTOR_BIASES + 1
PSUM_BANKS = 8
SAMPLES_IN_FLIGHT = 4

FLOPS = 2 * SAMPLES * P * P * NODES_OUT


def tile_fgl_kernel(tc, x, weight, mask_weight, ct_weight, ct_bias, bias, offs, out):
    nc = tc.nc
    with (
        tc.tile_pool(name="held", bufs=1) as held,
        tc.tile_pool(name="windows", bufs=2) as windows,
        tc.tile_pool(name="work", bufs=SAMPLES_IN_FLIGHT) as work,
        tc.tile_pool(name="results", bufs=SAMPLES + 1) as results,
        tc.tile_pool(name="msgs", bufs=(SAMPLES + 1) * NEIGHBOURS) as msgs,
        tc.psum_pool(name="sums", bufs=PSUM_BANKS - OUTPUT_BANKS) as sums,
        tc.psum_pool(name="outputs", bufs=OUTPUT_BANKS) as outputs,
    ):
        node_weight = held.tile([P, NODES_IN], F32, name="node_weight")
        nc.scalar.dma_start(node_weight[:], weight)
        x_all = held.tile([P, SAMPLES, NODES_IN], F32, name="x_all")
        nc.sync.dma_start(x_all[:, 0, :], x[0:P, :])
        offsets = held.tile([P, EDGES // OFFSETS_PER_COLUMN], U16, name="offsets")
        nc.sync.dma_start(offsets[:], offs)
        edge_weight = held.tile([P, EDGES], F32, name="edge_weight")
        for d in range(NEIGHBOURS):
            queue = nc.scalar if d % 2 == 0 else nc.sync
            piece = slice(d * NODES_OUT, (d + 1) * NODES_OUT)
            queue.dma_start(edge_weight[:, piece], mask_weight[:, piece].broadcast_to([P, NODES_OUT]))
        mix_weight = held.tile([P, P], BF16, name="mix_weight")
        nc.scalar.dma_start(mix_weight[:], ct_weight)
        node_bias = held.tile([P, NODES_OUT], F32, name="node_bias")
        nc.scalar.dma_start(node_bias[:], bias)
        channel_bias = held.tile([P, 1], F32, name="channel_bias")
        nc.scalar.dma_start(channel_bias[:], ct_bias)
        for first, last in ((1, 2), (2, 4), (4, SAMPLES)):
            rows = x[first * P : last * P, :].rearrange("(b p) s -> p b s", p=P)
            nc.sync.dma_start(x_all[:, first:last, :], rows)

        identity = held.tile([P, P], F32, name="identity")
        make_identity(nc, identity[:])

        for b in range(SAMPLES):
            feat = windows.tile([P, NODES_IN], F32, name="feat")
            nc.vector.tensor_tensor(feat[:], x_all[:, b, :], node_weight[:], MULT)

            halves = 2 if b == SAMPLES - 1 else 1
            width = NODES_OUT // halves
            for first in range(0, NODES_OUT, width):
                total = sums.tile([P, NODES_OUT], F32, name="total")
                for d in range(NEIGHBOURS):
                    entry = d * NODES_OUT + first
                    msg = msgs.tile([P, NODES_OUT], F32, name="msg")
                    looked_up = feat[:].indirect(
                        offsets[:, entry // OFFSETS_PER_COLUMN : (entry + width) // OFFSETS_PER_COLUMN]
                    )
                    nc.vector.tensor_tensor(msg[:, 0:width], looked_up, edge_weight[:, entry : entry + width], MULT)
                    nc.tensor.matmul(
                        total[:, 0:width], identity[:], msg[:, 0:width], start=(d == 0), stop=(d == NEIGHBOURS - 1)
                    )

                pooled = work.tile([P, NODES_OUT], BF16, name="pooled")
                nc.scalar.activation(pooled[:, 0:width], total[:, 0:width], COPY, scale=1.0 / NEIGHBOURS)

                mixed = outputs.tile([P, NODES_OUT], F32, name="mixed")
                result = results.tile([P, NODES_OUT], F32, name="result")
                nodes = slice(first, first + width)
                if b < SAMPLES - VECTOR_BIASES:
                    nc.tensor.matmul(mixed[:, 0:width], mix_weight[:], pooled[:, 0:width], start=True, stop=False)
                    nc.tensor.matmul(mixed[:, 0:width], identity[:], node_bias[:, nodes], start=False, stop=True)
                    nc.scalar.activation(result[:, 0:width], mixed[:, 0:width], IDENTITY, bias=channel_bias[:, 0:1])
                else:
                    nc.tensor.matmul(mixed[:, 0:width], mix_weight[:], pooled[:, 0:width], start=True, stop=True)
                    nc.vector.scalar_tensor_tensor(
                        result[:, 0:width], mixed[:, 0:width], channel_bias[:, 0:1], node_bias[:, nodes], ADD, ADD
                    )
                nc.sync.dma_start(out[b * P : (b + 1) * P, first : first + width], result[:, 0:width])
